import numpy as np
import ml_dtypes


def mxq(x, axis, fmt="e4m3"):
    dtype, down = {"e4m3": (ml_dtypes.float8_e4m3fn, 7), "e5m2": (ml_dtypes.float8_e5m2, 14)}[fmt]
    v = np.moveaxis(np.asarray(x, np.float32).astype(ml_dtypes.bfloat16).astype(np.float64), axis, -1)
    blocks = v.reshape(v.shape[:-1] + (-1, 32))
    amax = np.abs(blocks).max(-1, keepdims=True)
    byte = np.maximum(np.where(amax > 0, np.frexp(amax)[1] - 1 + 127, 0) - down, 1)
    scale = np.exp2(byte - 127.0)
    codes = (blocks / scale).astype(np.float32).astype(dtype).astype(np.float64)
    return np.moveaxis((codes * scale).reshape(v.shape), -1, axis)


WIDE = False


def mx_kscale(k):
    if not WIDE:
        return np.ones(k)
    levels = np.array([10, -10, 5, -5, 0])
    a = np.random.permutation(np.resize(levels, k // 512 * 4)).reshape(k // 512, 4)
    idx = np.arange(k)
    return np.exp2(a[idx // 512, idx % 128 // 32])


BF16 = ml_dtypes.bfloat16


def bf(x):
    return np.asarray(x, np.float32).astype(BF16)


def f64(x):
    return np.asarray(x).astype(np.float64)


B, IN_DIM, LAT, OUT_DIM = 384, 512, 1024, 512
G = IN_DIM + LAT


def sigmoid(v):
    return 1.0 / (1.0 + np.exp(-v))


def setup_inputs():
    s = mx_kscale(G)
    return {
        "x_t": bf(np.random.standard_normal((B, IN_DIM)) * s[:IN_DIM]),
        "h_t": bf(np.random.standard_normal((B, LAT)) * 0.85 * s[IN_DIM:]),
        "Wy": bf(np.random.standard_normal((G, OUT_DIM)) * 0.8 / np.sqrt(G) / s[:, None]),
        "by": bf(np.random.standard_normal(OUT_DIM) * 0.2),
        "Wo": bf(np.random.standard_normal((G, OUT_DIM)) * 0.8 / np.sqrt(G) / s[:, None]),
        "bo": bf(np.random.standard_normal(OUT_DIM) * 0.2),
    }


def reference(x_t, h_t, Wy, by, Wo, bo):
    xq = mxq(np.concatenate([f64(x_t), f64(h_t)], axis=1), 1, "e4m3")
    y_hat = np.tanh((xq @ mxq(f64(Wy), 0, "e4m3")) + f64(by))
    o_t = sigmoid((xq @ mxq(f64(Wo), 0, "e4m3")) + f64(bo))
    return y_hat * o_t

@@ -1,0 +1,209 @@
+from contextlib import ExitStack
+
+import concourse.mybir as mybir
+from concourse.masks import make_identity
+
+FLOPS = 2 * 384 * 1536 * 1024
+
+F32 = mybir.dt.float32
+BF16 = mybir.dt.bfloat16
+U32 = mybir.dt.uint32
+U8 = mybir.dt.uint8
+I32 = mybir.dt.int32
+FP8X4 = mybir.dt.float8_e4m3fn_x4
+ACT = mybir.ActivationFunctionType
+ALU = mybir.AluOpType
+
+P = 128
+PACK = 4
+K_PASS = P * PACK
+PASSES = 3
+BT = 3
+NT = 4
+N = 512
+COLS = BT * P
+S_NT = 3
+
+
+def tile_gatel0rdcell_pb_kernel(tc, x_t, h_t, Wy, by, Wo, bo, out):
+    nc = tc.nc
+    with ExitStack() as ctx:
+        keep = ctx.enter_context(tc.tile_pool(name="keep", bufs=1))
+        psa = ctx.enter_context(tc.psum_pool(name="psa", bufs=4))
+        psb = ctx.enter_context(tc.psum_pool(name="psb", bufs=4))
+
+        xt_sb = keep.tile([P, BT * 512], BF16, name="xt_sb")
+        ht_sb = keep.tile([P, BT * 1024], BF16, name="ht_sb")
+        raw = {}
+        for w in range(2):
+            for c in range(PASSES):
+                raw[(w, c)] = keep.tile([P, PACK, N], BF16, name="raw%d%d" % (w, c))
+
+        def load_w(w, c):
+            src = (Wy, Wo)[w]
+            nc.sync.dma_start(
+                out=raw[(w, c)][:],
+                in_=src[c * K_PASS:(c + 1) * K_PASS, :].rearrange("(p j) n -> p j n", j=PACK),
+            )
+
+        nc.sync.dma_start(out=xt_sb[:], in_=x_t.rearrange("(p t) k -> p (t k)", t=BT))
+        load_w(0, 0)
+        nc.sync.dma_start(out=ht_sb[:], in_=h_t.rearrange("(p t) k -> p (t k)", t=BT))
+        load_w(0, 1)
+        load_w(0, 2)
+        load_w(1, 0)
+        load_w(1, 1)
+        load_w(1, 2)
+
+        warm = keep.tile([P, 1], F32, name="warm")
+        nc.vector.memset(warm[:], 0.0)
+        nc.scalar.activation(out=warm[:], in_=warm[:], func=ACT.Sigmoid)
+
+        brow = keep.tile([P, P], BF16, name="brow")
+        nc.vector.memset(brow[:], 0.0)
+        nc.gpsimd.dma_start(out=brow[0:NT, :], in_=by.rearrange("(r c) -> r c", c=P))
+        nc.gpsimd.dma_start(out=brow[NT:2 * NT, :], in_=bo.rearrange("(r c) -> r c", c=P))
+        ident_f = keep.tile([P, P], F32, name="ident_f")
+        make_identity(nc, ident_f[:])
+        ident_b = keep.tile([P, P], BF16, name="ident_b")
+        make_identity(nc, ident_b[:])
+
+        xc = keep.tile([P, PASSES * N], U32, name="xc", align_bytes=64)
+        xs = keep.tile([P, PASSES * N], U8, name="xs", align_bytes=64)
+        nc.vector.memset(xc[:].bitcast(I32), 0)
+        nc.vector.memset(xs[:].bitcast(I32), 0)
+
+        xt_w = xt_sb[:].bitcast(F32)
+        ht_w = ht_sb[:].bitcast(F32)
+
+        xg = {}
+
+        def x_transpose(c):
+            xg[c] = keep.tile([P, COLS * PACK], BF16, name="xg%d" % c, align_bytes=64)
+            g32 = xg[c][:].bitcast(F32).rearrange("p (r u) -> p r u", u=2)
+            xa = psa.tile([P, 2, 2 * P], F32, tag="a", name="xa%d" % c)
+            xb = psa.tile([P, 2, P], F32, tag="a", name="xb%d" % c)
+            for t in range(BT):
+                for u in range(2):
+                    if c == 0:
+                        src = xt_w[:, t * 256 + u:(t + 1) * 256:2]
+                    else:
+                        lo = t * 512 + (c - 1) * 256
+                        src = ht_w[:, lo + u:lo + 256:2]
+                    dst = xa[:, u, t * P:(t + 1) * P] if t < 2 else xb[:, u, :]
+                    nc.tensor.transpose(out=dst, in_=src, identity=ident_f[:])
+            nc.scalar.copy(out=g32[:, 0:2 * P, :], in_=xa[:].rearrange("p u r -> p r u"))
+            nc.scalar.copy(out=g32[:, 2 * P:COLS, :], in_=xb[:].rearrange("p u r -> p r u"))
+
+        def x_quant(c):
+            for lo, hi in ((0, 2 * P), (2 * P, COLS)):
+                nc.vector.quantize_mx(
+                    out=xc[:, c * N + lo:c * N + hi].bitcast(FP8X4),
+                    scales=xs[:, c * N + lo:c * N + hi],
+                    in_=xg[c][:, lo * PACK:hi * PACK],
+                )
+
+        wg = {}
+        wc = {}
+        ws = {}
+
+        def w_regroup(w, c):
+            wg[(w, c)] = keep.tile([P, N * PACK], BF16, name="wg%d%d" % (w, c), align_bytes=64)
+            for eng, lo, hi in (("v", 0, S_NT * P), ("s", S_NT * P, N)):
+                dst = wg[(w, c)][:, lo * PACK:hi * PACK].rearrange("p (c i t) -> p c t i", i=4, t=PACK)
+                src = raw[(w, c)][:, :, lo:hi].rearrange("p t (c i) -> p c t i", i=4)
+                if eng == "v":
+                    nc.vector.tensor_copy(out=dst, in_=src)
+                else:
+                    nc.scalar.copy(out=dst, in_=src)
+
+        def w_quant(w, c):
+            wc[(w, c)] = keep.tile([P, N], U32, name="wc%d%d" % (w, c), align_bytes=64)
+            ws[(w, c)] = keep.tile([P, N], U8, name="ws%d%d" % (w, c), align_bytes=64)
+            for lo, hi in ((0, 2 * P), (2 * P, N)):
+                nc.vector.quantize_mx(
+                    out=wc[(w, c)][:, lo:hi].bitcast(FP8X4),
+                    scales=ws[(w, c)][:, lo:hi],
+                    in_=wg[(w, c)][:, lo * PACK:hi * PACK],
+                )
+
+        acc = {}
+
+        def mx(w, c):
+            for nt in range(NT):
+                if c == 0:
+                    pool, tag = ((psb, "b"), (psa, "a"))[w]
+                    acc[(w, nt)] = pool.tile([P, N], F32, tag=tag, name="acc%d%d" % (w, nt))
+                nc.tensor.matmul_mx(
+                    out=acc[(w, nt)][:],
+                    lhsT=wc[(w, c)][:, nt * P:(nt + 1) * P].bitcast(FP8X4),
+                    lhsT_scale=ws[(w, c)][:, nt * P:(nt + 1) * P],
+                    rhs=xc[:, c * N:(c + 1) * N].bitcast(FP8X4),
+                    rhs_scale=xs[:, c * N:(c + 1) * N],
+                    start=(c == 0),
+                    stop=(c == PASSES - 1),
+                )
+
+        bias = keep.tile([P, 2 * NT], F32, name="bias")
+
+        def bias_columns():
+            bps = psa.tile([P, P], BF16, tag="a", name="bps")
+            nc.tensor.transpose(out=bps[:], in_=brow[:], identity=ident_b[:])
+            nc.vector.tensor_copy(out=bias[:], in_=bps[:, 0:2 * NT])
+
+        def gate(w, nt):
+            g = keep.tile([P, COLS], F32, name="g%d%d" % (w, nt))
+            nc.scalar.activation(
+                out=g[:],
+                in_=acc[(w, nt)][:, 0:COLS],
+                func=(ACT.Tanh, ACT.Sigmoid)[w],
+                bias=bias[:, w * NT + nt:w * NT + nt + 1],
+                scale=1.0,
+            )
+            gp = psb.tile([P, BT, P], F32, tag="b", name="gp%d%d" % (w, nt))
+            for t in range(BT):
+                nc.tensor.transpose(out=gp[:, t, :], in_=g[:, t * P:(t + 1) * P], identity=ident_f[:])
+            return gp
+
+        out_v = out.rearrange("(p t) n -> p t n", t=BT)
+        ysb = {}
+
+        x_transpose(0)
+        w_regroup(0, 0)
+        x_quant(0)
+        bias_columns()
+        x_transpose(1)
+        w_quant(0, 0)
+        mx(0, 0)
+        x_transpose(2)
+        x_quant(1)
+        w_regroup(0, 1)
+        x_quant(2)
+        w_quant(0, 1)
+        mx(0, 1)
+        w_regroup(0, 2)
+        w_quant(0, 2)
+        mx(0, 2)
+        w_regroup(1, 0)
+        for nt in range(NT):
+            gp = gate(0, nt)
+            ysb[nt] = keep.tile([P, BT, P], F32, name="ysb%d" % nt)
+            if nt % 2 == 0:
+                nc.vector.tensor_copy(out=ysb[nt][:], in_=gp[:])
+            else:
+                nc.scalar.copy(out=ysb[nt][:], in_=gp[:])
+            if nt == 0:
+                w_quant(1, 0)
+                mx(1, 0)
+                w_regroup(1, 1)
+            if nt == 2:
+                w_quant(1, 1)
+                mx(1, 1)
+                w_regroup(1, 2)
+        w_quant(1, 2)
+        mx(1, 2)
+        for nt in range(NT):
+            gp = gate(1, nt)
+            res = keep.tile([P, BT, P], F32, name="res%d" % nt)
+            nc.vector.tensor_tensor(out=res[:], in0=gp[:], in1=ysb[nt][:], op=ALU.mult)
+            nc.sync.dma_start(out=out_v[:, :, nt * P:(nt + 1) * P], in_=res[:])

@@ -22,22 +22,121 @@ BT = 3
 NT = 4
 N = 512
 COLS = BT * P
-S_NT = 3
+
+STEPS = [
+    ("rg", "v", 0, 0, 0, 256),
+    ("rg", "s", 0, 0, 256, 512),
+    ("q", "v", 0, 0, 0, 256),
+    ("xT", "pe", 0, "A"),
+    ("xT", "pe", 0, "B"),
+    ("xe", "s", 0, "A"),
+    ("xe", "v", 0, "B"),
+    ("q", "v", 0, 0, 256, 512),
+    ("xq", "v", 0, "A"),
+    ("xT", "pe", 1, "A"),
+    ("xq", "v", 0, "B"),
+    ("bcast", "v"),
+    ("xT", "pe", 1, "B"),
+    ("xT", "pe", 2, "A"),
+    ("xe", "s", 1, "A"),
+    ("xe", "v", 1, "B"),
+    ("xT", "pe", 2, "B"),
+    ("bT", "pe"),
+    ("mx", "pe", 0, 0, 0),
+    ("xe", "s", 2, "A"),
+    ("xe", "v", 2, "B"),
+    ("mx", "pe", 0, 0, 1),
+    ("rg", "v", 0, 1, 0, 256),
+    ("mx", "pe", 0, 0, 2),
+    ("rg", "s", 0, 1, 384, 512),
+    ("mx", "pe", 0, 0, 3),
+    ("xq", "v", 1, "A"),
+    ("rg", "s", 0, 2, 384, 512),
+    ("xq", "v", 1, "B"),
+    ("rg", "v", 0, 1, 256, 384),
+    ("q", "v", 0, 1, 0, 256),
+    ("xq", "v", 2, "A"),
+    ("rg", "s", 1, 0, 256, 512),
+    ("xq", "v", 2, "B"),
+    ("bcopy", "v"),
+    ("mx", "pe", 0, 1, 0),
+    ("q", "v", 0, 1, 256, 512),
+    ("mx", "pe", 0, 1, 1),
+    ("rg", "v", 0, 2, 0, 256),
+    ("mx", "pe", 0, 1, 2),
+    ("rg", "s", 1, 1, 256, 512),
+    ("mx", "pe", 0, 1, 3),
+    ("rg", "v", 0, 2, 256, 384),
+    ("q", "v", 0, 2, 0, 256),
+    ("q", "v", 0, 2, 256, 512),
+    ("rg", "v", 1, 0, 0, 256),
+    ("mx", "pe", 0, 2, 0),
+    ("mx", "pe", 0, 2, 1),
+    ("mx", "pe", 0, 2, 2),
+    ("act", "s", 0, 0),
+    ("q", "v", 1, 0, 0, 256),
+    ("mx", "pe", 0, 2, 3),
+    ("q", "v", 1, 0, 256, 512),
+    ("act", "s", 0, 1),
+    ("rg", "v", 1, 1, 0, 256),
+    ("mx", "pe", 1, 0, 0),
+    ("mx", "pe", 1, 0, 1),
+    ("rg", "s", 1, 2, 256, 512),
+    ("mx", "pe", 1, 0, 2),
+    ("q", "v", 1, 1, 0, 256),
+    ("mx", "pe", 1, 0, 3),
+    ("q", "v", 1, 1, 256, 512),
+    ("rg", "v", 1, 2, 0, 256),
+    ("mx", "pe", 1, 1, 0),
+    ("act", "s", 0, 2),
+    ("mx", "pe", 1, 1, 1),
+    ("mx", "pe", 1, 1, 2),
+    ("q", "v", 1, 2, 0, 256),
+    ("act", "s", 0, 3),
+    ("mx", "pe", 1, 1, 3),
+    ("q", "v", 1, 2, 256, 512),
+    ("mx", "pe", 1, 2, 0),
+    ("mx", "pe", 1, 2, 1),
+    ("mx", "pe", 1, 2, 2),
+    ("act", "s", 1, 0),
+    ("mx", "pe", 1, 2, 3),
+    ("act", "s", 1, 1),
+    ("mul", "v", 0),
+    ("act", "s", 1, 2),
+    ("mul", "v", 1),
+    ("T", "pe", 0),
+    ("act", "s", 1, 3),
+    ("mul", "v", 2),
+    ("T", "pe", 1),
+    ("ex", "s", 0),
+    ("mul", "v", 3),
+    ("T", "pe", 2),
+    ("ex", "s", 1),
+    ("T", "pe", 3),
+    ("ex", "s", 2),
+    ("ex", "v", 3),
+]
 
 
 def tile_gatel0rdcell_pb_kernel(tc, x_t, h_t, Wy, by, Wo, bo, out):
     nc = tc.nc
     with ExitStack() as ctx:
         keep = ctx.enter_context(tc.tile_pool(name="keep", bufs=1))
-        psa = ctx.enter_context(tc.psum_pool(name="psa", bufs=4))
-        psb = ctx.enter_context(tc.psum_pool(name="psb", bufs=4))
+        psum = ctx.enter_context(tc.psum_pool(name="psum", bufs=1))
+        ctx.enter_context(tc.manual_schedule())
 
         xt_sb = keep.tile([P, BT * 512], BF16, name="xt_sb")
         ht_sb = keep.tile([P, BT * 1024], BF16, name="ht_sb")
         raw = {}
+        wg = {}
+        wc = {}
+        ws = {}
         for w in range(2):
             for c in range(PASSES):
                 raw[(w, c)] = keep.tile([P, PACK, N], BF16, name="raw%d%d" % (w, c))
+                wg[(w, c)] = keep.tile([P, N * PACK], BF16, name="wg%d%d" % (w, c), align_bytes=64)
+                wc[(w, c)] = keep.tile([P, N], U32, name="wc%d%d" % (w, c), align_bytes=64)
+                ws[(w, c)] = keep.tile([P, N], U8, name="ws%d%d" % (w, c), align_bytes=64)
 
         def load_w(w, c):
             src = (Wy, Wo)[w]
@@ -46,27 +145,30 @@ def tile_gatel0rdcell_pb_kernel(tc, x_t, h_t, Wy, by, Wo, bo, out):
                 in_=src[c * K_PASS:(c + 1) * K_PASS, :].rearrange("(p j) n -> p j n", j=PACK),
             )
 
-        nc.sync.dma_start(out=xt_sb[:], in_=x_t.rearrange("(p t) k -> p (t k)", t=BT))
+        def load_x():
+            nc.sync.dma_start(out=xt_sb[:], in_=x_t.rearrange("(p t) k -> p (t k)", t=BT))
+
+        def load_h():
+            nc.sync.dma_start(out=ht_sb[:], in_=h_t.rearrange("(p t) k -> p (t k)", t=BT))
+
         load_w(0, 0)
-        nc.sync.dma_start(out=ht_sb[:], in_=h_t.rearrange("(p t) k -> p (t k)", t=BT))
+        load_x()
+        load_h()
         load_w(0, 1)
         load_w(0, 2)
         load_w(1, 0)
         load_w(1, 1)
         load_w(1, 2)
 
+        brow = keep.tile([P, P], BF16, name="brow")
+        nc.vector.memset(brow[:], 0.0)
+        nc.scalar.dma_start(out=brow[0:NT, :], in_=by.rearrange("(r c) -> r c", c=P))
+        nc.scalar.dma_start(out=brow[NT:2 * NT, :], in_=bo.rearrange("(r c) -> r c", c=P))
         warm = keep.tile([P, 1], F32, name="warm")
         nc.vector.memset(warm[:], 0.0)
         nc.scalar.activation(out=warm[:], in_=warm[:], func=ACT.Sigmoid)
-
-        brow = keep.tile([P, P], BF16, name="brow")
-        nc.vector.memset(brow[:], 0.0)
-        nc.gpsimd.dma_start(out=brow[0:NT, :], in_=by.rearrange("(r c) -> r c", c=P))
-        nc.gpsimd.dma_start(out=brow[NT:2 * NT, :], in_=bo.rearrange("(r c) -> r c", c=P))
         ident_f = keep.tile([P, P], F32, name="ident_f")
         make_identity(nc, ident_f[:])
-        ident_b = keep.tile([P, P], BF16, name="ident_b")
-        make_identity(nc, ident_b[:])
 
         xc = keep.tile([P, PASSES * N], U32, name="xc", align_bytes=64)
         xs = keep.tile([P, PASSES * N], U8, name="xs", align_bytes=64)
@@ -75,135 +177,123 @@ def tile_gatel0rdcell_pb_kernel(tc, x_t, h_t, Wy, by, Wo, bo, out):
 
         xt_w = xt_sb[:].bitcast(F32)
         ht_w = ht_sb[:].bitcast(F32)
-
         xg = {}
-
-        def x_transpose(c):
+        for c in range(PASSES):
             xg[c] = keep.tile([P, COLS * PACK], BF16, name="xg%d" % c, align_bytes=64)
-            g32 = xg[c][:].bitcast(F32).rearrange("p (r u) -> p r u", u=2)
-            xa = psa.tile([P, 2, 2 * P], F32, tag="a", name="xa%d" % c)
-            xb = psa.tile([P, 2, P], F32, tag="a", name="xb%d" % c)
-            for t in range(BT):
+        xps = {}
+        x_bank = {(0, "A"): 4, (0, "B"): 5, (1, "A"): 6, (1, "B"): 7, (2, "A"): 4, (2, "B"): 5}
+        x_cols = {"A": (0, 2 * P), "B": (2 * P, COLS)}
+
+        def copy(eng, dst, src):
+            if eng == "v":
+                nc.vector.tensor_copy(out=dst, in_=src)
+            else:
+                nc.scalar.copy(out=dst, in_=src)
+
+        def x_transpose(c, part):
+            lo, hi = x_cols[part]
+            tl = psum.tile([P, 2, hi - lo], F32, tag="k%d" % x_bank[(c, part)], name="xps%d%s" % (c, part))
+            xps[(c, part)] = tl
+            for t in range(lo // P, hi // P):
                 for u in range(2):
                     if c == 0:
                         src = xt_w[:, t * 256 + u:(t + 1) * 256:2]
                     else:
-                        lo = t * 512 + (c - 1) * 256
-                        src = ht_w[:, lo + u:lo + 256:2]
-                    dst = xa[:, u, t * P:(t + 1) * P] if t < 2 else xb[:, u, :]
-                    nc.tensor.transpose(out=dst, in_=src, identity=ident_f[:])
-            nc.scalar.copy(out=g32[:, 0:2 * P, :], in_=xa[:].rearrange("p u r -> p r u"))
-            nc.scalar.copy(out=g32[:, 2 * P:COLS, :], in_=xb[:].rearrange("p u r -> p r u"))
+                        base = t * 512 + (c - 1) * 256
+                        src = ht_w[:, base + u:base + 256:2]
+                    nc.tensor.transpose(out=tl[:, u, t * P - lo:(t + 1) * P - lo], in_=src, identity=ident_f[:])
 
-        def x_quant(c):
-            for lo, hi in ((0, 2 * P), (2 * P, COLS)):
-                nc.vector.quantize_mx(
-                    out=xc[:, c * N + lo:c * N + hi].bitcast(FP8X4),
-                    scales=xs[:, c * N + lo:c * N + hi],
-                    in_=xg[c][:, lo * PACK:hi * PACK],
-                )
+        def x_exit(eng, c, part):
+            lo, hi = x_cols[part]
+            g32 = xg[c][:].bitcast(F32).rearrange("p (r u) -> p r u", u=2)
+            copy(eng, g32[:, lo:hi, :], xps[(c, part)][:].rearrange("p u r -> p r u"))
 
-        wg = {}
-        wc = {}
-        ws = {}
+        def x_quant(c, part):
+            lo, hi = x_cols[part]
+            nc.vector.quantize_mx(
+                out=xc[:, c * N + lo:c * N + hi].bitcast(FP8X4),
+                scales=xs[:, c * N + lo:c * N + hi],
+                in_=xg[c][:, lo * PACK:hi * PACK],
+            )
 
-        def w_regroup(w, c):
-            wg[(w, c)] = keep.tile([P, N * PACK], BF16, name="wg%d%d" % (w, c), align_bytes=64)
-            for eng, lo, hi in (("v", 0, S_NT * P), ("s", S_NT * P, N)):
-                dst = wg[(w, c)][:, lo * PACK:hi * PACK].rearrange("p (c i t) -> p c t i", i=4, t=PACK)
-                src = raw[(w, c)][:, :, lo:hi].rearrange("p t (c i) -> p c t i", i=4)
-                if eng == "v":
-                    nc.vector.tensor_copy(out=dst, in_=src)
-                else:
-                    nc.scalar.copy(out=dst, in_=src)
+        def w_regroup(eng, w, c, lo, hi):
+            dst = wg[(w, c)][:, lo * PACK:hi * PACK].rearrange("p (c i t) -> p c t i", i=4, t=PACK)
+            src = raw[(w, c)][:, :, lo:hi].rearrange("p t (c i) -> p c t i", i=4)
+            copy(eng, dst, src)
 
-        def w_quant(w, c):
-            wc[(w, c)] = keep.tile([P, N], U32, name="wc%d%d" % (w, c), align_bytes=64)
-            ws[(w, c)] = keep.tile([P, N], U8, name="ws%d%d" % (w, c), align_bytes=64)
-            for lo, hi in ((0, 2 * P), (2 * P, N)):
-                nc.vector.quantize_mx(
-                    out=wc[(w, c)][:, lo:hi].bitcast(FP8X4),
-                    scales=ws[(w, c)][:, lo:hi],
-                    in_=wg[(w, c)][:, lo * PACK:hi * PACK],
-                )
+        def w_quant(w, c, lo, hi):
+            nc.vector.quantize_mx(
+                out=wc[(w, c)][:, lo:hi].bitcast(FP8X4),
+                scales=ws[(w, c)][:, lo:hi],
+                in_=wg[(w, c)][:, lo * PACK:hi * PACK],
+            )
 
         acc = {}
 
-        def mx(w, c):
-            for nt in range(NT):
-                if c == 0:
-                    pool, tag = ((psb, "b"), (psa, "a"))[w]
-                    acc[(w, nt)] = pool.tile([P, N], F32, tag=tag, name="acc%d%d" % (w, nt))
-                nc.tensor.matmul_mx(
-                    out=acc[(w, nt)][:],
-                    lhsT=wc[(w, c)][:, nt * P:(nt + 1) * P].bitcast(FP8X4),
-                    lhsT_scale=ws[(w, c)][:, nt * P:(nt + 1) * P],
-                    rhs=xc[:, c * N:(c + 1) * N].bitcast(FP8X4),
-                    rhs_scale=xs[:, c * N:(c + 1) * N],
-                    start=(c == 0),
-                    stop=(c == PASSES - 1),
-                )
-
-        bias = keep.tile([P, 2 * NT], F32, name="bias")
-
-        def bias_columns():
-            bps = psa.tile([P, P], BF16, tag="a", name="bps")
-            nc.tensor.transpose(out=bps[:], in_=brow[:], identity=ident_b[:])
-            nc.vector.tensor_copy(out=bias[:], in_=bps[:, 0:2 * NT])
-
-        def gate(w, nt):
-            g = keep.tile([P, COLS], F32, name="g%d%d" % (w, nt))
-            nc.scalar.activation(
-                out=g[:],
-                in_=acc[(w, nt)][:, 0:COLS],
-                func=(ACT.Tanh, ACT.Sigmoid)[w],
-                bias=bias[:, w * NT + nt:w * NT + nt + 1],
-                scale=1.0,
+        def mx(w, c, nt):
+            if c == 0:
+                acc[(w, nt)] = psum.tile([P, N], F32, tag="k%d" % (w * NT + nt), name="acc%d%d" % (w, nt))
+            nc.tensor.matmul_mx(
+                out=acc[(w, nt)][:],
+                lhsT=wc[(w, c)][:, nt * P:(nt + 1) * P].bitcast(FP8X4),
+                lhsT_scale=ws[(w, c)][:, nt * P:(nt + 1) * P],
+                rhs=xc[:, c * N:(c + 1) * N].bitcast(FP8X4),
+                rhs_scale=xs[:, c * N:(c + 1) * N],
+                start=(c == 0),
+                stop=(c == PASSES - 1),
             )
-            gp = psb.tile([P, BT, P], F32, tag="b", name="gp%d%d" % (w, nt))
-            for t in range(BT):
-                nc.tensor.transpose(out=gp[:, t, :], in_=g[:, t * P:(t + 1) * P], identity=ident_f[:])
-            return gp
 
+        brow_f = keep.tile([P, P], F32, name="brow_f")
+        bias = keep.tile([P, 2 * NT], F32, name="bias")
+        bps = {}
+        gate = {}
+        prod = {}
+        pt = {}
         out_v = out.rearrange("(p t) n -> p t n", t=BT)
-        ysb = {}
 
-        x_transpose(0)
-        w_regroup(0, 0)
-        x_quant(0)
-        bias_columns()
-        x_transpose(1)
-        w_quant(0, 0)
-        mx(0, 0)
-        x_transpose(2)
-        x_quant(1)
-        w_regroup(0, 1)
-        x_quant(2)
-        w_quant(0, 1)
-        mx(0, 1)
-        w_regroup(0, 2)
-        w_quant(0, 2)
-        mx(0, 2)
-        w_regroup(1, 0)
-        for nt in range(NT):
-            gp = gate(0, nt)
-            ysb[nt] = keep.tile([P, BT, P], F32, name="ysb%d" % nt)
-            if nt % 2 == 0:
-                nc.vector.tensor_copy(out=ysb[nt][:], in_=gp[:])
-            else:
-                nc.scalar.copy(out=ysb[nt][:], in_=gp[:])
-            if nt == 0:
-                w_quant(1, 0)
-                mx(1, 0)
-                w_regroup(1, 1)
-            if nt == 2:
-                w_quant(1, 1)
-                mx(1, 1)
-                w_regroup(1, 2)
-        w_quant(1, 2)
-        mx(1, 2)
-        for nt in range(NT):
-            gp = gate(1, nt)
-            res = keep.tile([P, BT, P], F32, name="res%d" % nt)
-            nc.vector.tensor_tensor(out=res[:], in0=gp[:], in1=ysb[nt][:], op=ALU.mult)
-            nc.sync.dma_start(out=out_v[:, :, nt * P:(nt + 1) * P], in_=res[:])
+        for step in STEPS:
+            kind = step[0]
+            eng = step[1]
+            if kind == "rg":
+                w_regroup(eng, step[2], step[3], step[4], step[5])
+            elif kind == "q":
+                w_quant(step[2], step[3], step[4], step[5])
+            elif kind == "xT":
+                x_transpose(step[2], step[3])
+            elif kind == "xe":
+                x_exit(eng, step[2], step[3])
+            elif kind == "xq":
+                x_quant(step[2], step[3])
+            elif kind == "mx":
+                mx(step[2], step[3], step[4])
+            elif kind == "bcast":
+                nc.vector.tensor_copy(out=brow_f[:], in_=brow[:])
+            elif kind == "bT":
+                bps[0] = psum.tile([P, P], F32, tag="k6", name="bps")
+                nc.tensor.transpose(out=bps[0][:], in_=brow_f[:], identity=ident_f[:])
+            elif kind == "bcopy":
+                nc.vector.tensor_copy(out=bias[:], in_=bps[0][:, 0:2 * NT])
+            elif kind == "act":
+                w, nt = step[2], step[3]
+                gate[(w, nt)] = keep.tile([P, COLS], F32, name="gate%d%d" % (w, nt))
+                nc.scalar.activation(
+                    out=gate[(w, nt)][:],
+                    in_=acc[(w, nt)][:, 0:COLS],
+                    func=(ACT.Tanh, ACT.Sigmoid)[w],
+                    bias=bias[:, w * NT + nt:w * NT + nt + 1],
+                    scale=1.0,
+                )
+            elif kind == "mul":
+                nt = step[2]
+                prod[nt] = keep.tile([P, COLS], F32, name="prod%d" % nt)
+                nc.vector.tensor_tensor(out=prod[nt][:], in0=gate[(0, nt)][:], in1=gate[(1, nt)][:], op=ALU.mult)
+            elif kind == "T":
+                nt = step[2]
+                pt[nt] = psum.tile([P, BT, P], F32, tag="k%d" % nt, name="pt%d" % nt)
+                for t in range(BT):
+                    nc.tensor.transpose(out=pt[nt][:, t, :], in_=prod[nt][:, t * P:(t + 1) * P], identity=ident_f[:])
+            elif kind == "ex":
+                nt = step[2]
+                res = keep.tile([P, BT, P], F32, name="res%d" % nt)
+                copy(eng, res[:], pt[nt][:])
+                nc.sync.dma_start(out=out_v[:, :, nt * P:(nt + 1) * P], in_=res[:])

@@ -24,97 +24,101 @@ N = 512
 COLS = BT * P
 
 STEPS = [
-    ("rg", "v", 0, 0, 0, 256),
-    ("rg", "s", 0, 0, 256, 512),
-    ("q", "v", 0, 0, 0, 256),
+    ("rg", "s", 0, 0, 0, 128),
+    ("rg", "v", 0, 0, 128, 384),
+    ("rg", "s", 0, 0, 384, 512),
     ("xT", "pe", 0, "A"),
+    ("q", "v", 0, 0, 0, 256),
     ("xT", "pe", 0, "B"),
-    ("xe", "s", 0, "A"),
-    ("xe", "v", 0, "B"),
+    ("xe", "v", 0, "A"),
+    ("xe", "s", 0, "B"),
     ("q", "v", 0, 0, 256, 512),
+    ("xT", "pe", 1, "B"),
     ("xq", "v", 0, "A"),
-    ("xT", "pe", 1, "A"),
+    ("xT", "pe", 2, "B"),
     ("xq", "v", 0, "B"),
     ("bcast", "v"),
-    ("xT", "pe", 1, "B"),
-    ("xT", "pe", 2, "A"),
-    ("xe", "s", 1, "A"),
-    ("xe", "v", 1, "B"),
-    ("xT", "pe", 2, "B"),
-    ("bT", "pe"),
-    ("mx", "pe", 0, 0, 0),
-    ("xe", "s", 2, "A"),
-    ("xe", "v", 2, "B"),
-    ("mx", "pe", 0, 0, 1),
-    ("rg", "v", 0, 1, 0, 256),
-    ("mx", "pe", 0, 0, 2),
-    ("rg", "s", 0, 1, 384, 512),
-    ("mx", "pe", 0, 0, 3),
-    ("xq", "v", 1, "A"),
-    ("rg", "s", 0, 2, 384, 512),
+    ("xe", "s", 1, "B"),
+    ("xT", "pe", 1, "A"),
+    ("xe", "s", 2, "B"),
     ("xq", "v", 1, "B"),
-    ("rg", "v", 0, 1, 256, 384),
-    ("q", "v", 0, 1, 0, 256),
-    ("xq", "v", 2, "A"),
-    ("rg", "s", 1, 0, 256, 512),
+    ("rg", "v", 0, 1, 128, 512),
+    ("rg", "s", 0, 1, 0, 128),
+    ("xT", "pe", 2, "A"),
+    ("bT", "pe"),
+    ("xe", "s", 1, "A"),
+    ("mx", "pe", 0, 0, 1),
     ("xq", "v", 2, "B"),
-    ("bcopy", "v"),
-    ("mx", "pe", 0, 1, 0),
     ("q", "v", 0, 1, 256, 512),
-    ("mx", "pe", 0, 1, 1),
-    ("rg", "v", 0, 2, 0, 256),
-    ("mx", "pe", 0, 1, 2),
-    ("rg", "s", 1, 1, 256, 512),
-    ("mx", "pe", 0, 1, 3),
-    ("rg", "v", 0, 2, 256, 384),
+    ("rg", "s", 0, 2, 128, 256),
+    ("mx", "pe", 0, 0, 2),
+    ("rg", "v", 0, 2, 0, 128),
+    ("q", "v", 0, 1, 0, 256),
+    ("xe", "s", 2, "A"),
+    ("mx", "pe", 0, 0, 0),
+    ("xq", "v", 1, "A"),
     ("q", "v", 0, 2, 0, 256),
+    ("rg", "s", 0, 2, 256, 384),
+    ("mx", "pe", 0, 0, 3),
+    ("xq", "v", 2, "A"),
+    ("bcopy", "v"),
+    ("rg", "s", 1, 0, 0, 128),
+    ("rg", "v", 0, 2, 384, 512),
+    ("mx", "pe", 0, 1, 2),
+    ("rg", "v", 1, 0, 384, 512),
+    ("rg", "s", 1, 1, 256, 512),
+    ("mx", "pe", 0, 1, 0),
     ("q", "v", 0, 2, 256, 512),
-    ("rg", "v", 1, 0, 0, 256),
-    ("mx", "pe", 0, 2, 0),
-    ("mx", "pe", 0, 2, 1),
-    ("mx", "pe", 0, 2, 2),
-    ("act", "s", 0, 0),
-    ("q", "v", 1, 0, 0, 256),
-    ("mx", "pe", 0, 2, 3),
-    ("q", "v", 1, 0, 256, 512),
-    ("act", "s", 0, 1),
+    ("mx", "pe", 0, 1, 3),
+    ("rg", "v", 1, 0, 128, 256),
+    ("mx", "pe", 0, 1, 1),
     ("rg", "v", 1, 1, 0, 256),
-    ("mx", "pe", 1, 0, 0),
-    ("mx", "pe", 1, 0, 1),
-    ("rg", "s", 1, 2, 256, 512),
-    ("mx", "pe", 1, 0, 2),
+    ("mx", "pe", 0, 2, 3),
+    ("rg", "s", 1, 0, 256, 384),
+    ("mx", "pe", 0, 2, 2),
+    ("q", "v", 1, 0, 0, 256),
+    ("mx", "pe", 0, 2, 0),
     ("q", "v", 1, 1, 0, 256),
-    ("mx", "pe", 1, 0, 3),
-    ("q", "v", 1, 1, 256, 512),
-    ("rg", "v", 1, 2, 0, 256),
-    ("mx", "pe", 1, 1, 0),
+    ("rg", "s", 1, 2, 128, 256),
+    ("mx", "pe", 0, 2, 1),
+    ("q", "v", 1, 0, 256, 512),
+    ("mx", "pe", 1, 0, 0),
+    ("rg", "v", 1, 2, 0, 128),
+    ("mx", "pe", 1, 0, 1),
     ("act", "s", 0, 2),
+    ("mx", "pe", 1, 1, 0),
+    ("q", "v", 1, 1, 256, 512),
+    ("act", "s", 0, 1),
     ("mx", "pe", 1, 1, 1),
-    ("mx", "pe", 1, 1, 2),
     ("q", "v", 1, 2, 0, 256),
+    ("mx", "pe", 1, 0, 3),
+    ("rg", "v", 1, 2, 256, 512),
+    ("act", "s", 0, 0),
+    ("mx", "pe", 1, 0, 2),
+    ("mx", "pe", 1, 2, 0),
     ("act", "s", 0, 3),
     ("mx", "pe", 1, 1, 3),
     ("q", "v", 1, 2, 256, 512),
-    ("mx", "pe", 1, 2, 0),
     ("mx", "pe", 1, 2, 1),
-    ("mx", "pe", 1, 2, 2),
     ("act", "s", 1, 0),
+    ("mx", "pe", 1, 1, 2),
     ("mx", "pe", 1, 2, 3),
-    ("act", "s", 1, 1),
     ("mul", "v", 0),
-    ("act", "s", 1, 2),
+    ("act", "s", 1, 1),
+    ("mx", "pe", 1, 2, 2),
     ("mul", "v", 1),
-    ("T", "pe", 0),
     ("act", "s", 1, 3),
-    ("mul", "v", 2),
+    ("T", "pe", 0),
+    ("act", "s", 1, 2),
     ("T", "pe", 1),
-    ("ex", "s", 0),
     ("mul", "v", 3),
-    ("T", "pe", 2),
+    ("mul", "v", 2),
     ("ex", "s", 1),
     ("T", "pe", 3),
-    ("ex", "s", 2),
+    ("ex", "v", 0),
+    ("T", "pe", 2),
     ("ex", "v", 3),
+    ("ex", "s", 2),
 ]
 
 
@@ -141,8 +145,8 @@ def tile_gatel0rdcell_pb_kernel(tc, x_t, h_t, Wy, by, Wo, bo, out):
         def load_w(w, c):
             src = (Wy, Wo)[w]
             nc.sync.dma_start(
-                out=raw[(w, c)][:],
-                in_=src[c * K_PASS:(c + 1) * K_PASS, :].rearrange("(p j) n -> p j n", j=PACK),
+                out=raw[(w, c)][:].rearrange("p (u e) n -> p u (e n)", u=2),
+                in_=src[c * K_PASS:(c + 1) * K_PASS, :].rearrange("(u p e) n -> p u (e n)", u=2, e=2),
             )
 
         def load_x():
@@ -197,10 +201,10 @@ def tile_gatel0rdcell_pb_kernel(tc, x_t, h_t, Wy, by, Wo, bo, out):
             for t in range(lo // P, hi // P):
                 for u in range(2):
                     if c == 0:
-                        src = xt_w[:, t * 256 + u:(t + 1) * 256:2]
+                        src = xt_w[:, t * 256 + u * P:t * 256 + (u + 1) * P]
                     else:
                         base = t * 512 + (c - 1) * 256
-                        src = ht_w[:, base + u:base + 256:2]
+                        src = ht_w[:, base + u * P:base + (u + 1) * P]
                     nc.tensor.transpose(out=tl[:, u, t * P - lo:(t + 1) * P - lo], in_=src, identity=ident_f[:])
 
         def x_exit(eng, c, part):
@@ -269,7 +273,7 @@ def tile_gatel0rdcell_pb_kernel(tc, x_t, h_t, Wy, by, Wo, bo, out):
             elif kind == "bcast":
                 nc.vector.tensor_copy(out=brow_f[:], in_=brow[:])
             elif kind == "bT":
-                bps[0] = psum.tile([P, P], F32, tag="k6", name="bps")
+                bps[0] = psum.tile([P, P], F32, tag="k7", name="bps")
                 nc.tensor.transpose(out=bps[0][:], in_=brow_f[:], identity=ident_f[:])
             elif kind == "bcopy":
                 nc.vector.tensor_copy(out=bias[:], in_=bps[0][:, 0:2 * NT])

@@ -127,7 +127,6 @@ def tile_gatel0rdcell_pb_kernel(tc, x_t, h_t, Wy, by, Wo, bo, out):
     with ExitStack() as ctx:
         keep = ctx.enter_context(tc.tile_pool(name="keep", bufs=1))
         psum = ctx.enter_context(tc.psum_pool(name="psum", bufs=1))
-        ctx.enter_context(tc.manual_schedule())
 
         xt_sb = keep.tile([P, BT * 512], BF16, name="xt_sb")
         ht_sb = keep.tile([P, BT * 1024], BF16, name="ht_sb")

@@ -18,285 +18,240 @@ P = 128
 PACK = 4
 K_PASS = P * PACK
 PASSES = 3
-BT = 3
-NT = 4
-N = 512
-COLS = BT * P
+ROWS = 3
+BATCH = ROWS * P
+TILES = 4
+N_OUT = TILES * P
+N_MOVING = 512
+WORDS = K_PASS // 2
+RUN = 4
+TANH = 0
+SIGMOID = 1
 
-STEPS = [
-    ("rg", "s", 0, 0, 0, 128),
-    ("rg", "v", 0, 0, 128, 384),
-    ("rg", "s", 0, 0, 384, 512),
-    ("xT", "pe", 0, "A"),
-    ("q", "v", 0, 0, 0, 256),
-    ("xT", "pe", 0, "B"),
-    ("xe", "v", 0, "A"),
-    ("xe", "s", 0, "B"),
-    ("q", "v", 0, 0, 256, 512),
-    ("xT", "pe", 1, "B"),
-    ("xq", "v", 0, "A"),
-    ("xT", "pe", 2, "B"),
-    ("xq", "v", 0, "B"),
-    ("bcast", "v"),
-    ("xe", "s", 1, "B"),
-    ("xT", "pe", 1, "A"),
-    ("xe", "s", 2, "B"),
-    ("xq", "v", 1, "B"),
-    ("rg", "v", 0, 1, 128, 512),
-    ("rg", "s", 0, 1, 0, 128),
-    ("xT", "pe", 2, "A"),
-    ("bT", "pe"),
-    ("xe", "s", 1, "A"),
-    ("mx", "pe", 0, 0, 1),
-    ("xq", "v", 2, "B"),
-    ("q", "v", 0, 1, 256, 512),
-    ("rg", "s", 0, 2, 128, 256),
-    ("mx", "pe", 0, 0, 2),
-    ("rg", "v", 0, 2, 0, 128),
-    ("q", "v", 0, 1, 0, 256),
-    ("xe", "s", 2, "A"),
-    ("mx", "pe", 0, 0, 0),
-    ("xq", "v", 1, "A"),
-    ("q", "v", 0, 2, 0, 256),
-    ("rg", "s", 0, 2, 256, 384),
-    ("mx", "pe", 0, 0, 3),
-    ("xq", "v", 2, "A"),
-    ("bcopy", "v"),
-    ("rg", "s", 1, 0, 0, 128),
-    ("rg", "v", 0, 2, 384, 512),
-    ("mx", "pe", 0, 1, 2),
-    ("rg", "v", 1, 0, 384, 512),
-    ("rg", "s", 1, 1, 256, 512),
-    ("mx", "pe", 0, 1, 0),
-    ("q", "v", 0, 2, 256, 512),
-    ("mx", "pe", 0, 1, 3),
-    ("rg", "v", 1, 0, 128, 256),
-    ("mx", "pe", 0, 1, 1),
-    ("rg", "v", 1, 1, 0, 256),
-    ("mx", "pe", 0, 2, 3),
-    ("rg", "s", 1, 0, 256, 384),
-    ("mx", "pe", 0, 2, 2),
-    ("q", "v", 1, 0, 0, 256),
-    ("mx", "pe", 0, 2, 0),
-    ("q", "v", 1, 1, 0, 256),
-    ("rg", "s", 1, 2, 128, 256),
-    ("mx", "pe", 0, 2, 1),
-    ("q", "v", 1, 0, 256, 512),
-    ("mx", "pe", 1, 0, 0),
-    ("rg", "v", 1, 2, 0, 128),
-    ("mx", "pe", 1, 0, 1),
-    ("act", "s", 0, 2),
-    ("mx", "pe", 1, 1, 0),
-    ("q", "v", 1, 1, 256, 512),
-    ("act", "s", 0, 1),
-    ("mx", "pe", 1, 1, 1),
-    ("q", "v", 1, 2, 0, 256),
-    ("mx", "pe", 1, 0, 3),
-    ("rg", "v", 1, 2, 256, 512),
-    ("act", "s", 0, 0),
-    ("mx", "pe", 1, 0, 2),
-    ("mx", "pe", 1, 2, 0),
-    ("act", "s", 0, 3),
-    ("mx", "pe", 1, 1, 3),
-    ("q", "v", 1, 2, 256, 512),
-    ("mx", "pe", 1, 2, 1),
-    ("act", "s", 1, 0),
-    ("mx", "pe", 1, 1, 2),
-    ("mx", "pe", 1, 2, 3),
-    ("mul", "v", 0),
-    ("act", "s", 1, 1),
-    ("mx", "pe", 1, 2, 2),
-    ("mul", "v", 1),
-    ("act", "s", 1, 3),
-    ("T", "pe", 0),
-    ("act", "s", 1, 2),
-    ("T", "pe", 1),
-    ("mul", "v", 3),
-    ("mul", "v", 2),
-    ("ex", "s", 1),
-    ("T", "pe", 3),
-    ("ex", "v", 0),
-    ("T", "pe", 2),
-    ("ex", "v", 3),
-    ("ex", "s", 2),
-]
+X_COLUMNS = {"A": (0, 2 * P), "B": (2 * P, BATCH)}
+X_BANK = {(0, "A"): 4, (0, "B"): 5, (1, "A"): 6, (1, "B"): 7, (2, "A"): 4, (2, "B"): 5}
+BIAS_BANK = 7
 
 
 def tile_gatel0rdcell_pb_kernel(tc, x_t, h_t, Wy, by, Wo, bo, out):
     nc = tc.nc
+    on_vector = nc.vector.tensor_copy
+    on_scalar = nc.scalar.copy
     with ExitStack() as ctx:
         keep = ctx.enter_context(tc.tile_pool(name="keep", bufs=1))
         psum = ctx.enter_context(tc.psum_pool(name="psum", bufs=1))
+        ctx.enter_context(tc.manual_schedule())
 
-        xt_sb = keep.tile([P, BT * 512], BF16, name="xt_sb")
-        ht_sb = keep.tile([P, BT * 1024], BF16, name="ht_sb")
-        raw = {}
-        wg = {}
-        wc = {}
-        ws = {}
-        for w in range(2):
+        xt_sb = keep.tile([P, ROWS * K_PASS], BF16, name="xt_sb")
+        ht_sb = keep.tile([P, ROWS * 2 * K_PASS], BF16, name="ht_sb")
+        w_rows = {}
+        w_grouped = {}
+        w_codes = {}
+        w_scales = {}
+        for g in (TANH, SIGMOID):
             for c in range(PASSES):
-                raw[(w, c)] = keep.tile([P, PACK, N], BF16, name="raw%d%d" % (w, c))
-                wg[(w, c)] = keep.tile([P, N * PACK], BF16, name="wg%d%d" % (w, c), align_bytes=64)
-                wc[(w, c)] = keep.tile([P, N], U32, name="wc%d%d" % (w, c), align_bytes=64)
-                ws[(w, c)] = keep.tile([P, N], U8, name="ws%d%d" % (w, c), align_bytes=64)
+                w_rows[(g, c)] = keep.tile([P, PACK, N_OUT], BF16, name="w_rows%d%d" % (g, c))
+                w_grouped[(g, c)] = keep.tile([P, N_OUT * PACK], BF16, name="w_grouped%d%d" % (g, c), align_bytes=64)
+                w_codes[(g, c)] = keep.tile([P, N_OUT], U32, name="w_codes%d%d" % (g, c), align_bytes=64)
+                w_scales[(g, c)] = keep.tile([P, N_OUT], U8, name="w_scales%d%d" % (g, c), align_bytes=64)
 
-        def load_w(w, c):
-            src = (Wy, Wo)[w]
+        def load_weights(g, c):
+            rows = (Wy, Wo)[g][c * K_PASS:(c + 1) * K_PASS, :]
             nc.sync.dma_start(
-                out=raw[(w, c)][:].rearrange("p (u e) n -> p u (e n)", u=2),
-                in_=src[c * K_PASS:(c + 1) * K_PASS, :].rearrange("(u p e) n -> p u (e n)", u=2, e=2),
+                out=w_rows[(g, c)][:].rearrange("p (u e) n -> p u (e n)", u=2),
+                in_=rows.rearrange("(u p e) n -> p u (e n)", u=2, e=2),
             )
 
-        def load_x():
-            nc.sync.dma_start(out=xt_sb[:], in_=x_t.rearrange("(p t) k -> p (t k)", t=BT))
+        load_weights(TANH, 0)
+        nc.sync.dma_start(out=xt_sb[:], in_=x_t.rearrange("(p t) k -> p (t k)", t=ROWS))
+        nc.sync.dma_start(out=ht_sb[:], in_=h_t.rearrange("(p t) k -> p (t k)", t=ROWS))
+        load_weights(TANH, 1)
+        load_weights(TANH, 2)
+        load_weights(SIGMOID, 0)
+        load_weights(SIGMOID, 1)
+        load_weights(SIGMOID, 2)
 
-        def load_h():
-            nc.sync.dma_start(out=ht_sb[:], in_=h_t.rearrange("(p t) k -> p (t k)", t=BT))
-
-        load_w(0, 0)
-        load_x()
-        load_h()
-        load_w(0, 1)
-        load_w(0, 2)
-        load_w(1, 0)
-        load_w(1, 1)
-        load_w(1, 2)
-
-        brow = keep.tile([P, P], BF16, name="brow")
-        nc.vector.memset(brow[:], 0.0)
-        nc.scalar.dma_start(out=brow[0:NT, :], in_=by.rearrange("(r c) -> r c", c=P))
-        nc.scalar.dma_start(out=brow[NT:2 * NT, :], in_=bo.rearrange("(r c) -> r c", c=P))
+        bias_rows = keep.tile([P, P], BF16, name="bias_rows")
+        nc.vector.memset(bias_rows[:], 0.0)
+        nc.scalar.dma_start(out=bias_rows[0:TILES, :], in_=by.rearrange("(r c) -> r c", c=P))
+        nc.scalar.dma_start(out=bias_rows[TILES:2 * TILES, :], in_=bo.rearrange("(r c) -> r c", c=P))
         warm = keep.tile([P, 1], F32, name="warm")
         nc.vector.memset(warm[:], 0.0)
         nc.scalar.activation(out=warm[:], in_=warm[:], func=ACT.Sigmoid)
-        ident_f = keep.tile([P, P], F32, name="ident_f")
-        make_identity(nc, ident_f[:])
+        identity = keep.tile([P, P], F32, name="identity")
+        make_identity(nc, identity[:])
+        x_codes = keep.tile([P, PASSES * N_MOVING], U32, name="x_codes", align_bytes=64)
+        x_scales = keep.tile([P, PASSES * N_MOVING], U8, name="x_scales", align_bytes=64)
+        nc.vector.memset(x_codes[:].bitcast(I32), 0)
+        nc.vector.memset(x_scales[:].bitcast(I32), 0)
 
-        xc = keep.tile([P, PASSES * N], U32, name="xc", align_bytes=64)
-        xs = keep.tile([P, PASSES * N], U8, name="xs", align_bytes=64)
-        nc.vector.memset(xc[:].bitcast(I32), 0)
-        nc.vector.memset(xs[:].bitcast(I32), 0)
-
-        xt_w = xt_sb[:].bitcast(F32)
-        ht_w = ht_sb[:].bitcast(F32)
-        xg = {}
+        xt_words = xt_sb[:].bitcast(F32)
+        ht_words = ht_sb[:].bitcast(F32)
+        x_grouped = {}
         for c in range(PASSES):
-            xg[c] = keep.tile([P, COLS * PACK], BF16, name="xg%d" % c, align_bytes=64)
-        xps = {}
-        x_bank = {(0, "A"): 4, (0, "B"): 5, (1, "A"): 6, (1, "B"): 7, (2, "A"): 4, (2, "B"): 5}
-        x_cols = {"A": (0, 2 * P), "B": (2 * P, COLS)}
+            x_grouped[c] = keep.tile([P, BATCH * PACK], BF16, name="x_grouped%d" % c, align_bytes=64)
+        x_psum = {}
 
-        def copy(eng, dst, src):
-            if eng == "v":
-                nc.vector.tensor_copy(out=dst, in_=src)
-            else:
-                nc.scalar.copy(out=dst, in_=src)
-
-        def x_transpose(c, part):
-            lo, hi = x_cols[part]
-            tl = psum.tile([P, 2, hi - lo], F32, tag="k%d" % x_bank[(c, part)], name="xps%d%s" % (c, part))
-            xps[(c, part)] = tl
+        def transpose_x(c, part):
+            lo, hi = X_COLUMNS[part]
+            x_psum[(c, part)] = psum.tile([P, 2, hi - lo], F32, tag="bank%d" % X_BANK[(c, part)], name="x_psum%d%s" % (c, part))
             for t in range(lo // P, hi // P):
                 for u in range(2):
                     if c == 0:
-                        src = xt_w[:, t * 256 + u * P:t * 256 + (u + 1) * P]
+                        first = t * WORDS + u * P
+                        words = xt_words[:, first:first + P]
                     else:
-                        base = t * 512 + (c - 1) * 256
-                        src = ht_w[:, base + u * P:base + (u + 1) * P]
-                    nc.tensor.transpose(out=tl[:, u, t * P - lo:(t + 1) * P - lo], in_=src, identity=ident_f[:])
+                        first = t * 2 * WORDS + (c - 1) * WORDS + u * P
+                        words = ht_words[:, first:first + P]
+                    nc.tensor.transpose(out=x_psum[(c, part)][:, u, t * P - lo:(t + 1) * P - lo], in_=words, identity=identity[:])
 
-        def x_exit(eng, c, part):
-            lo, hi = x_cols[part]
-            g32 = xg[c][:].bitcast(F32).rearrange("p (r u) -> p r u", u=2)
-            copy(eng, g32[:, lo:hi, :], xps[(c, part)][:].rearrange("p u r -> p r u"))
+        def copy_x(copy, c, part):
+            lo, hi = X_COLUMNS[part]
+            grouped_words = x_grouped[c][:].bitcast(F32).rearrange("p (r u) -> p r u", u=2)
+            copy(out=grouped_words[:, lo:hi, :], in_=x_psum[(c, part)][:].rearrange("p u r -> p r u"))
 
-        def x_quant(c, part):
-            lo, hi = x_cols[part]
+        def quantise_x(c, part):
+            lo, hi = X_COLUMNS[part]
             nc.vector.quantize_mx(
-                out=xc[:, c * N + lo:c * N + hi].bitcast(FP8X4),
-                scales=xs[:, c * N + lo:c * N + hi],
-                in_=xg[c][:, lo * PACK:hi * PACK],
+                out=x_codes[:, c * N_MOVING + lo:c * N_MOVING + hi].bitcast(FP8X4),
+                scales=x_scales[:, c * N_MOVING + lo:c * N_MOVING + hi],
+                in_=x_grouped[c][:, lo * PACK:hi * PACK],
             )
 
-        def w_regroup(eng, w, c, lo, hi):
-            dst = wg[(w, c)][:, lo * PACK:hi * PACK].rearrange("p (c i t) -> p c t i", i=4, t=PACK)
-            src = raw[(w, c)][:, :, lo:hi].rearrange("p t (c i) -> p c t i", i=4)
-            copy(eng, dst, src)
+        def regroup(copy, g, c, first_tile, end_tile):
+            lo, hi = first_tile * P, end_tile * P
+            copy(
+                out=w_grouped[(g, c)][:, lo * PACK:hi * PACK].rearrange("p (a i j) -> p a j i", i=RUN, j=PACK),
+                in_=w_rows[(g, c)][:, :, lo:hi].rearrange("p j (a i) -> p a j i", i=RUN),
+            )
 
-        def w_quant(w, c, lo, hi):
+        def quantise_weights(g, c, h):
+            lo, hi = h * 2 * P, (h + 1) * 2 * P
             nc.vector.quantize_mx(
-                out=wc[(w, c)][:, lo:hi].bitcast(FP8X4),
-                scales=ws[(w, c)][:, lo:hi],
-                in_=wg[(w, c)][:, lo * PACK:hi * PACK],
+                out=w_codes[(g, c)][:, lo:hi].bitcast(FP8X4),
+                scales=w_scales[(g, c)][:, lo:hi],
+                in_=w_grouped[(g, c)][:, lo * PACK:hi * PACK],
             )
 
-        acc = {}
+        sums = {}
 
-        def mx(w, c, nt):
-            if c == 0:
-                acc[(w, nt)] = psum.tile([P, N], F32, tag="k%d" % (w * NT + nt), name="acc%d%d" % (w, nt))
-            nc.tensor.matmul_mx(
-                out=acc[(w, nt)][:],
-                lhsT=wc[(w, c)][:, nt * P:(nt + 1) * P].bitcast(FP8X4),
-                lhsT_scale=ws[(w, c)][:, nt * P:(nt + 1) * P],
-                rhs=xc[:, c * N:(c + 1) * N].bitcast(FP8X4),
-                rhs_scale=xs[:, c * N:(c + 1) * N],
-                start=(c == 0),
-                stop=(c == PASSES - 1),
-            )
-
-        brow_f = keep.tile([P, P], F32, name="brow_f")
-        bias = keep.tile([P, 2 * NT], F32, name="bias")
-        bps = {}
-        gate = {}
-        prod = {}
-        pt = {}
-        out_v = out.rearrange("(p t) n -> p t n", t=BT)
-
-        for step in STEPS:
-            kind = step[0]
-            eng = step[1]
-            if kind == "rg":
-                w_regroup(eng, step[2], step[3], step[4], step[5])
-            elif kind == "q":
-                w_quant(step[2], step[3], step[4], step[5])
-            elif kind == "xT":
-                x_transpose(step[2], step[3])
-            elif kind == "xe":
-                x_exit(eng, step[2], step[3])
-            elif kind == "xq":
-                x_quant(step[2], step[3])
-            elif kind == "mx":
-                mx(step[2], step[3], step[4])
-            elif kind == "bcast":
-                nc.vector.tensor_copy(out=brow_f[:], in_=brow[:])
-            elif kind == "bT":
-                bps[0] = psum.tile([P, P], F32, tag="k7", name="bps")
-                nc.tensor.transpose(out=bps[0][:], in_=brow_f[:], identity=ident_f[:])
-            elif kind == "bcopy":
-                nc.vector.tensor_copy(out=bias[:], in_=bps[0][:, 0:2 * NT])
-            elif kind == "act":
-                w, nt = step[2], step[3]
-                gate[(w, nt)] = keep.tile([P, COLS], F32, name="gate%d%d" % (w, nt))
-                nc.scalar.activation(
-                    out=gate[(w, nt)][:],
-                    in_=acc[(w, nt)][:, 0:COLS],
-                    func=(ACT.Tanh, ACT.Sigmoid)[w],
-                    bias=bias[:, w * NT + nt:w * NT + nt + 1],
-                    scale=1.0,
+        def multiply(g, c, first_tile, end_tile):
+            for n in range(first_tile, end_tile):
+                if c == 0:
+                    sums[(g, n)] = psum.tile([P, N_MOVING], F32, tag="bank%d" % (g * TILES + n), name="sums%d%d" % (g, n))
+                nc.tensor.matmul_mx(
+                    out=sums[(g, n)][:],
+                    lhsT=w_codes[(g, c)][:, n * P:(n + 1) * P].bitcast(FP8X4),
+                    lhsT_scale=w_scales[(g, c)][:, n * P:(n + 1) * P],
+                    rhs=x_codes[:, c * N_MOVING:(c + 1) * N_MOVING].bitcast(FP8X4),
+                    rhs_scale=x_scales[:, c * N_MOVING:(c + 1) * N_MOVING],
+                    start=(c == 0),
+                    stop=(c == PASSES - 1),
                 )
-            elif kind == "mul":
-                nt = step[2]
-                prod[nt] = keep.tile([P, COLS], F32, name="prod%d" % nt)
-                nc.vector.tensor_tensor(out=prod[nt][:], in0=gate[(0, nt)][:], in1=gate[(1, nt)][:], op=ALU.mult)
-            elif kind == "T":
-                nt = step[2]
-                pt[nt] = psum.tile([P, BT, P], F32, tag="k%d" % nt, name="pt%d" % nt)
-                for t in range(BT):
-                    nc.tensor.transpose(out=pt[nt][:, t, :], in_=prod[nt][:, t * P:(t + 1) * P], identity=ident_f[:])
-            elif kind == "ex":
-                nt = step[2]
-                res = keep.tile([P, BT, P], F32, name="res%d" % nt)
-                copy(eng, res[:], pt[nt][:])
-                nc.sync.dma_start(out=out_v[:, :, nt * P:(nt + 1) * P], in_=res[:])
+
+        bias_rows_f32 = keep.tile([P, P], F32, name="bias_rows_f32")
+        bias = keep.tile([P, 2 * TILES], F32, name="bias")
+        gates = {}
+        products = {}
+        products_psum = {}
+        out_view = out.rearrange("(p t) n -> p t n", t=ROWS)
+
+        def gate(g, n):
+            gates[(g, n)] = keep.tile([P, BATCH], F32, name="gates%d%d" % (g, n))
+            nc.scalar.activation(
+                out=gates[(g, n)][:],
+                in_=sums[(g, n)][:, 0:BATCH],
+                func=(ACT.Tanh, ACT.Sigmoid)[g],
+                bias=bias[:, g * TILES + n:g * TILES + n + 1],
+                scale=1.0,
+            )
+
+        def product(n):
+            products[n] = keep.tile([P, BATCH], F32, name="products%d" % n)
+            nc.vector.tensor_tensor(out=products[n][:], in0=gates[(TANH, n)][:], in1=gates[(SIGMOID, n)][:], op=ALU.mult)
+
+        def transpose_product(n):
+            products_psum[n] = psum.tile([P, ROWS, P], F32, tag="bank%d" % n, name="products_psum%d" % n)
+            for t in range(ROWS):
+                nc.tensor.transpose(out=products_psum[n][:, t, :], in_=products[n][:, t * P:(t + 1) * P], identity=identity[:])
+
+        def store(copy, n):
+            result = keep.tile([P, ROWS, P], F32, name="result%d" % n)
+            copy(out=result[:], in_=products_psum[n][:])
+            nc.sync.dma_start(out=out_view[:, :, n * P:(n + 1) * P], in_=result[:])
+
+
+        regroup(on_scalar, TANH, 0, 0, 1)
+        regroup(on_vector, TANH, 0, 1, 3)
+        regroup(on_scalar, TANH, 0, 3, 4)
+        transpose_x(0, "A")
+        transpose_x(0, "B")
+        quantise_weights(TANH, 0, 0)
+        copy_x(on_vector, 0, "A")
+        copy_x(on_scalar, 0, "B")
+        quantise_weights(TANH, 0, 1)
+        quantise_x(0, "A")
+        quantise_x(0, "B")
+        nc.vector.tensor_copy(out=bias_rows_f32[:], in_=bias_rows[:])
+
+        transpose_x(1, "B")
+        transpose_x(2, "B")
+        transpose_x(1, "A")
+        transpose_x(2, "A")
+        copy_x(on_scalar, 1, "B")
+        bias_psum = psum.tile([P, P], F32, tag="bank%d" % BIAS_BANK, name="bias_psum")
+        nc.tensor.transpose(out=bias_psum[:], in_=bias_rows_f32[:], identity=identity[:])
+        copy_x(on_scalar, 2, "B")
+        quantise_x(1, "B")
+        regroup(on_vector, TANH, 1, 1, 4)
+        regroup(on_scalar, TANH, 1, 0, 1)
+        copy_x(on_scalar, 1, "A")
+        quantise_x(2, "B")
+        quantise_weights(TANH, 1, 1)
+        regroup(on_scalar, TANH, 2, 1, 2)
+        regroup(on_vector, TANH, 2, 0, 1)
+        quantise_weights(TANH, 1, 0)
+        copy_x(on_scalar, 2, "A")
+        quantise_x(1, "A")
+        quantise_weights(TANH, 2, 0)
+        regroup(on_scalar, TANH, 2, 2, 3)
+        quantise_x(2, "A")
+        nc.vector.tensor_copy(out=bias[:], in_=bias_psum[:, 0:2 * TILES])
+        multiply(TANH, 0, 0, TILES)
+        multiply(TANH, 1, 0, TILES)
+        regroup(on_vector, TANH, 2, 3, 4)
+
+        regroup(on_scalar, SIGMOID, 0, 0, 1)
+        regroup(on_vector, SIGMOID, 0, 3, 4)
+        regroup(on_scalar, SIGMOID, 1, 2, 4)
+        quantise_weights(TANH, 2, 1)
+        multiply(TANH, 2, 0, TILES)
+        regroup(on_vector, SIGMOID, 0, 1, 2)
+        regroup(on_vector, SIGMOID, 1, 0, 2)
+        regroup(on_scalar, SIGMOID, 0, 2, 3)
+        quantise_weights(SIGMOID, 0, 0)
+        quantise_weights(SIGMOID, 1, 0)
+        regroup(on_scalar, SIGMOID, 2, 1, 2)
+        quantise_weights(SIGMOID, 0, 1)
+        multiply(SIGMOID, 0, 0, 2)
+        multiply(SIGMOID, 1, 0, 2)
+        multiply(SIGMOID, 0, 2, TILES)
+        regroup(on_vector, SIGMOID, 2, 0, 1)
+        quantise_weights(SIGMOID, 1, 1)
+        quantise_weights(SIGMOID, 2, 0)
+        regroup(on_vector, SIGMOID, 2, 2, 4)
+        for n in range(TILES):
+            gate(TANH, n)
+        multiply(SIGMOID, 2, 0, 2)
+        multiply(SIGMOID, 1, 2, TILES)
+        quantise_weights(SIGMOID, 2, 1)
+        multiply(SIGMOID, 2, 2, TILES)
+
+        for n in range(TILES):
+            gate(SIGMOID, n)
+            product(n)
+            transpose_product(n)
+        store(on_scalar, 0)
+        store(on_scalar, 1)
+        store(on_vector, 2)
+        store(on_vector, 3)

@@ -192,15 +192,12 @@ def tile_gatel0rdcell_pb_kernel(tc, x_t, h_t, Wy, by, Wo, bo, out):
         quantise_weights(TANH, 0, 1)
         quantise_x(0, "A")
         quantise_x(0, "B")
-        nc.vector.tensor_copy(out=bias_rows_f32[:], in_=bias_rows[:])
 
         transpose_x(1, "B")
         transpose_x(2, "B")
         transpose_x(1, "A")
         transpose_x(2, "A")
         copy_x(on_scalar, 1, "B")
-        bias_psum = psum.tile([P, P], F32, tag="bank%d" % BIAS_BANK, name="bias_psum")
-        nc.tensor.transpose(out=bias_psum[:], in_=bias_rows_f32[:], identity=identity[:])
         copy_x(on_scalar, 2, "B")
         quantise_x(1, "B")
         regroup(on_vector, TANH, 1, 1, 4)
@@ -212,11 +209,11 @@ def tile_gatel0rdcell_pb_kernel(tc, x_t, h_t, Wy, by, Wo, bo, out):
         regroup(on_vector, TANH, 2, 0, 1)
         quantise_weights(TANH, 1, 0)
         copy_x(on_scalar, 2, "A")
+        nc.scalar.copy(out=bias_rows_f32[:], in_=bias_rows[:])
         quantise_x(1, "A")
         quantise_weights(TANH, 2, 0)
         regroup(on_scalar, TANH, 2, 2, 3)
         quantise_x(2, "A")
-        nc.vector.tensor_copy(out=bias[:], in_=bias_psum[:, 0:2 * TILES])
         multiply(TANH, 0, 0, TILES)
         multiply(TANH, 1, 0, TILES)
         regroup(on_vector, TANH, 2, 3, 4)
@@ -226,12 +223,15 @@ def tile_gatel0rdcell_pb_kernel(tc, x_t, h_t, Wy, by, Wo, bo, out):
         regroup(on_scalar, SIGMOID, 1, 2, 4)
         quantise_weights(TANH, 2, 1)
         multiply(TANH, 2, 0, TILES)
+        bias_psum = psum.tile([P, P], F32, tag="bank%d" % BIAS_BANK, name="bias_psum")
+        nc.tensor.transpose(out=bias_psum[:], in_=bias_rows_f32[:], identity=identity[:])
         regroup(on_vector, SIGMOID, 0, 1, 2)
         regroup(on_vector, SIGMOID, 1, 0, 2)
         regroup(on_scalar, SIGMOID, 0, 2, 3)
         quantise_weights(SIGMOID, 0, 0)
         quantise_weights(SIGMOID, 1, 0)
         regroup(on_scalar, SIGMOID, 2, 1, 2)
+        nc.scalar.copy(out=bias[:], in_=bias_psum[:, 0:2 * TILES])
         quantise_weights(SIGMOID, 0, 1)
         multiply(SIGMOID, 0, 0, 2)
         multiply(SIGMOID, 1, 0, 2)

@@ -181,9 +181,8 @@ def tile_gatel0rdcell_pb_kernel(tc, x_t, h_t, Wy, by, Wo, bo, out):
             nc.sync.dma_start(out=out_view[:, :, n * P:(n + 1) * P], in_=result[:])
 
 
-        regroup(on_scalar, TANH, 0, 0, 1)
-        regroup(on_vector, TANH, 0, 1, 3)
-        regroup(on_scalar, TANH, 0, 3, 4)
+        regroup(on_vector, TANH, 0, 0, 2)
+        regroup(on_scalar, TANH, 0, 2, 4)
         transpose_x(0, "A")
         transpose_x(0, "B")
         quantise_weights(TANH, 0, 0)
@@ -200,46 +199,42 @@ def tile_gatel0rdcell_pb_kernel(tc, x_t, h_t, Wy, by, Wo, bo, out):
         copy_x(on_scalar, 1, "B")
         copy_x(on_scalar, 2, "B")
         quantise_x(1, "B")
-        regroup(on_vector, TANH, 1, 1, 4)
-        regroup(on_scalar, TANH, 1, 0, 1)
-        copy_x(on_scalar, 1, "A")
+        regroup(on_vector, TANH, 1, 0, 3)
+        regroup(on_scalar, TANH, 1, 3, 4)
         quantise_x(2, "B")
-        quantise_weights(TANH, 1, 1)
-        regroup(on_scalar, TANH, 2, 1, 2)
-        regroup(on_vector, TANH, 2, 0, 1)
         quantise_weights(TANH, 1, 0)
-        copy_x(on_scalar, 2, "A")
-        nc.scalar.copy(out=bias_rows_f32[:], in_=bias_rows[:])
+        copy_x(on_scalar, 1, "A")
+        regroup(on_vector, TANH, 2, 0, 2)
+        regroup(on_scalar, TANH, 2, 2, 4)
+        quantise_weights(TANH, 1, 1)
         quantise_x(1, "A")
         quantise_weights(TANH, 2, 0)
-        regroup(on_scalar, TANH, 2, 2, 3)
+        copy_x(on_scalar, 2, "A")
+        nc.scalar.copy(out=bias_rows_f32[:], in_=bias_rows[:])
         quantise_x(2, "A")
         multiply(TANH, 0, 0, TILES)
         multiply(TANH, 1, 0, TILES)
-        regroup(on_vector, TANH, 2, 3, 4)
 
-        regroup(on_scalar, SIGMOID, 0, 0, 1)
-        regroup(on_vector, SIGMOID, 0, 3, 4)
-        regroup(on_scalar, SIGMOID, 1, 2, 4)
+        regroup(on_vector, SIGMOID, 0, 0, 2)
+        regroup(on_scalar, SIGMOID, 0, 2, 4)
         quantise_weights(TANH, 2, 1)
         multiply(TANH, 2, 0, TILES)
         bias_psum = psum.tile([P, P], F32, tag="bank%d" % BIAS_BANK, name="bias_psum")
         nc.tensor.transpose(out=bias_psum[:], in_=bias_rows_f32[:], identity=identity[:])
-        regroup(on_vector, SIGMOID, 0, 1, 2)
         regroup(on_vector, SIGMOID, 1, 0, 2)
-        regroup(on_scalar, SIGMOID, 0, 2, 3)
+        regroup(on_scalar, SIGMOID, 1, 2, 4)
         quantise_weights(SIGMOID, 0, 0)
         quantise_weights(SIGMOID, 1, 0)
-        regroup(on_scalar, SIGMOID, 2, 1, 2)
-        nc.scalar.copy(out=bias[:], in_=bias_psum[:, 0:2 * TILES])
         quantise_weights(SIGMOID, 0, 1)
+        regroup(on_scalar, SIGMOID, 2, 3, 4)
+        nc.scalar.copy(out=bias[:], in_=bias_psum[:, 0:2 * TILES])
         multiply(SIGMOID, 0, 0, 2)
         multiply(SIGMOID, 1, 0, 2)
         multiply(SIGMOID, 0, 2, TILES)
-        regroup(on_vector, SIGMOID, 2, 0, 1)
+        regroup(on_vector, SIGMOID, 2, 0, 2)
         quantise_weights(SIGMOID, 1, 1)
         quantise_weights(SIGMOID, 2, 0)
-        regroup(on_vector, SIGMOID, 2, 2, 4)
+        regroup(on_vector, SIGMOID, 2, 2, 3)
         for n in range(TILES):
             gate(TANH, n)
         multiply(SIGMOID, 2, 0, 2)

from contextlib import ExitStack

import concourse.mybir as mybir
from concourse.masks import make_identity

FLOPS = 2 * 384 * 1536 * 1024

F32 = mybir.dt.float32
BF16 = mybir.dt.bfloat16
U32 = mybir.dt.uint32
U8 = mybir.dt.uint8
I32 = mybir.dt.int32
FP8X4 = mybir.dt.float8_e4m3fn_x4
ACT = mybir.ActivationFunctionType
ALU = mybir.AluOpType

P = 128
PACK = 4
K_PASS = P * PACK
PASSES = 3
ROWS = 3
BATCH = ROWS * P
TILES = 4
N_OUT = TILES * P
N_MOVING = 512
WORDS = K_PASS // 2
RUN = 4
TANH = 0
SIGMOID = 1

X_COLUMNS = {"A": (0, 2 * P), "B": (2 * P, BATCH)}
X_BANK = {(0, "A"): 4, (0, "B"): 5, (1, "A"): 6, (1, "B"): 7, (2, "A"): 4, (2, "B"): 5}
BIAS_BANK = 7


def tile_gatel0rdcell_pb_kernel(tc, x_t, h_t, Wy, by, Wo, bo, out):
    nc = tc.nc
    on_vector = nc.vector.tensor_copy
    on_scalar = nc.scalar.copy
    with ExitStack() as ctx:
        keep = ctx.enter_context(tc.tile_pool(name="keep", bufs=1))
        psum = ctx.enter_context(tc.psum_pool(name="psum", bufs=1))
        ctx.enter_context(tc.manual_schedule())

        xt_sb = keep.tile([P, ROWS * K_PASS], BF16, name="xt_sb")
        ht_sb = keep.tile([P, ROWS * 2 * K_PASS], BF16, name="ht_sb")
        w_rows = {}
        w_grouped = {}
        w_codes = {}
        w_scales = {}
        for g in (TANH, SIGMOID):
            for c in range(PASSES):
                w_rows[(g, c)] = keep.tile([P, PACK, N_OUT], BF16, name="w_rows%d%d" % (g, c))
                w_grouped[(g, c)] = keep.tile([P, N_OUT * PACK], BF16, name="w_grouped%d%d" % (g, c), align_bytes=64)
                w_codes[(g, c)] = keep.tile([P, N_OUT], U32, name="w_codes%d%d" % (g, c), align_bytes=64)
                w_scales[(g, c)] = keep.tile([P, N_OUT], U8, name="w_scales%d%d" % (g, c), align_bytes=64)

        def load_weights(g, c):
            rows = (Wy, Wo)[g][c * K_PASS:(c + 1) * K_PASS, :]
            nc.sync.dma_start(
                out=w_rows[(g, c)][:].rearrange("p (u e) n -> p u (e n)", u=2),
                in_=rows.rearrange("(u p e) n -> p u (e n)", u=2, e=2),
            )

        load_weights(TANH, 0)
        nc.sync.dma_start(out=xt_sb[:], in_=x_t.rearrange("(p t) k -> p (t k)", t=ROWS))
        nc.sync.dma_start(out=ht_sb[:], in_=h_t.rearrange("(p t) k -> p (t k)", t=ROWS))
        load_weights(TANH, 1)
        load_weights(TANH, 2)
        load_weights(SIGMOID, 0)
        load_weights(SIGMOID, 1)
        load_weights(SIGMOID, 2)

        bias_rows = keep.tile([P, P], BF16, name="bias_rows")
        nc.vector.memset(bias_rows[:], 0.0)
        nc.scalar.dma_start(out=bias_rows[0:TILES, :], in_=by.rearrange("(r c) -> r c", c=P))
        nc.scalar.dma_start(out=bias_rows[TILES:2 * TILES, :], in_=bo.rearrange("(r c) -> r c", c=P))
        warm = keep.tile([P, 1], F32, name="warm")
        nc.vector.memset(warm[:], 0.0)
        nc.scalar.activation(out=warm[:], in_=warm[:], func=ACT.Sigmoid)
        identity = keep.tile([P, P], F32, name="identity")
        make_identity(nc, identity[:])
        x_codes = keep.tile([P, PASSES * N_MOVING], U32, name="x_codes", align_bytes=64)
        x_scales = keep.tile([P, PASSES * N_MOVING], U8, name="x_scales", align_bytes=64)
        nc.vector.memset(x_codes[:].bitcast(I32), 0)
        nc.vector.memset(x_scales[:].bitcast(I32), 0)

        xt_words = xt_sb[:].bitcast(F32)
        ht_words = ht_sb[:].bitcast(F32)
        x_grouped = {}
        for c in range(PASSES):
            x_grouped[c] = keep.tile([P, BATCH * PACK], BF16, name="x_grouped%d" % c, align_bytes=64)
        x_psum = {}

        def transpose_x(c, part):
            lo, hi = X_COLUMNS[part]
            x_psum[(c, part)] = psum.tile([P, 2, hi - lo], F32, tag="bank%d" % X_BANK[(c, part)], name="x_psum%d%s" % (c, part))
            for t in range(lo // P, hi // P):
                for u in range(2):
                    if c == 0:
                        first = t * WORDS + u * P
                        words = xt_words[:, first:first + P]
                    else:
                        first = t * 2 * WORDS + (c - 1) * WORDS + u * P
                        words = ht_words[:, first:first + P]
                    nc.tensor.transpose(out=x_psum[(c, part)][:, u, t * P - lo:(t + 1) * P - lo], in_=words, identity=identity[:])

        def copy_x(copy, c, part):
            lo, hi = X_COLUMNS[part]
            grouped_words = x_grouped[c][:].bitcast(F32).rearrange("p (r u) -> p r u", u=2)
            copy(out=grouped_words[:, lo:hi, :], in_=x_psum[(c, part)][:].rearrange("p u r -> p r u"))

        def quantise_x(c, part):
            lo, hi = X_COLUMNS[part]
            nc.vector.quantize_mx(
                out=x_codes[:, c * N_MOVING + lo:c * N_MOVING + hi].bitcast(FP8X4),
                scales=x_scales[:, c * N_MOVING + lo:c * N_MOVING + hi],
                in_=x_grouped[c][:, lo * PACK:hi * PACK],
            )

        def regroup(copy, g, c, first_tile, end_tile):
            lo, hi = first_tile * P, end_tile * P
            copy(
                out=w_grouped[(g, c)][:, lo * PACK:hi * PACK].rearrange("p (a i j) -> p a j i", i=RUN, j=PACK),
                in_=w_rows[(g, c)][:, :, lo:hi].rearrange("p j (a i) -> p a j i", i=RUN),
            )

        def quantise_weights(g, c, h):
            lo, hi = h * 2 * P, (h + 1) * 2 * P
            nc.vector.quantize_mx(
                out=w_codes[(g, c)][:, lo:hi].bitcast(FP8X4),
                scales=w_scales[(g, c)][:, lo:hi],
                in_=w_grouped[(g, c)][:, lo * PACK:hi * PACK],
            )

        sums = {}

        def multiply(g, c, first_tile, end_tile):
            for n in range(first_tile, end_tile):
                if c == 0:
                    sums[(g, n)] = psum.tile([P, N_MOVING], F32, tag="bank%d" % (g * TILES + n), name="sums%d%d" % (g, n))
                nc.tensor.matmul_mx(
                    out=sums[(g, n)][:],
                    lhsT=w_codes[(g, c)][:, n * P:(n + 1) * P].bitcast(FP8X4),
                    lhsT_scale=w_scales[(g, c)][:, n * P:(n + 1) * P],
                    rhs=x_codes[:, c * N_MOVING:(c + 1) * N_MOVING].bitcast(FP8X4),
                    rhs_scale=x_scales[:, c * N_MOVING:(c + 1) * N_MOVING],
                    start=(c == 0),
                    stop=(c == PASSES - 1),
                )

        bias_rows_f32 = keep.tile([P, P], F32, name="bias_rows_f32")
        bias = keep.tile([P, 2 * TILES], F32, name="bias")
        gates = {}
        products = {}
        products_psum = {}
        out_view = out.rearrange("(p t) n -> p t n", t=ROWS)

        def gate(g, n):
            gates[(g, n)] = keep.tile([P, BATCH], F32, name="gates%d%d" % (g, n))
            nc.scalar.activation(
                out=gates[(g, n)][:],
                in_=sums[(g, n)][:, 0:BATCH],
                func=(ACT.Tanh, ACT.Sigmoid)[g],
                bias=bias[:, g * TILES + n:g * TILES + n + 1],
                scale=1.0,
            )

        def product(n):
            products[n] = keep.tile([P, BATCH], F32, name="products%d" % n)
            nc.vector.tensor_tensor(out=products[n][:], in0=gates[(TANH, n)][:], in1=gates[(SIGMOID, n)][:], op=ALU.mult)

        def transpose_product(n):
            products_psum[n] = psum.tile([P, ROWS, P], F32, tag="bank%d" % n, name="products_psum%d" % n)
            for t in range(ROWS):
                nc.tensor.transpose(out=products_psum[n][:, t, :], in_=products[n][:, t * P:(t + 1) * P], identity=identity[:])

        def store(copy, n):
            result = keep.tile([P, ROWS, P], F32, name="result%d" % n)
            copy(out=result[:], in_=products_psum[n][:])
            nc.sync.dma_start(out=out_view[:, :, n * P:(n + 1) * P], in_=result[:])


        regroup(on_vector, TANH, 0, 0, 2)
        regroup(on_scalar, TANH, 0, 2, 4)
        transpose_x(0, "A")
        transpose_x(0, "B")
        quantise_weights(TANH, 0, 0)
        copy_x(on_vector, 0, "A")
        copy_x(on_scalar, 0, "B")
        quantise_weights(TANH, 0, 1)
        quantise_x(0, "A")
        quantise_x(0, "B")

        transpose_x(1, "B")
        transpose_x(2, "B")
        transpose_x(1, "A")
        transpose_x(2, "A")
        copy_x(on_scalar, 1, "B")
        copy_x(on_scalar, 2, "B")
        quantise_x(1, "B")
        regroup(on_vector, TANH, 1, 0, 3)
        regroup(on_scalar, TANH, 1, 3, 4)
        quantise_x(2, "B")
        quantise_weights(TANH, 1, 0)
        copy_x(on_scalar, 1, "A")
        regroup(on_vector, TANH, 2, 0, 2)
        regroup(on_scalar, TANH, 2, 2, 4)
        quantise_weights(TANH, 1, 1)
        quantise_x(1, "A")
        quantise_weights(TANH, 2, 0)
        copy_x(on_scalar, 2, "A")
        nc.scalar.copy(out=bias_rows_f32[:], in_=bias_rows[:])
        quantise_x(2, "A")
        multiply(TANH, 0, 0, TILES)
        multiply(TANH, 1, 0, TILES)

        regroup(on_vector, SIGMOID, 0, 0, 2)
        regroup(on_scalar, SIGMOID, 0, 2, 4)
        quantise_weights(TANH, 2, 1)
        multiply(TANH, 2, 0, TILES)
        bias_psum = psum.tile([P, P], F32, tag="bank%d" % BIAS_BANK, name="bias_psum")
        nc.tensor.transpose(out=bias_psum[:], in_=bias_rows_f32[:], identity=identity[:])
        regroup(on_vector, SIGMOID, 1, 0, 2)
        regroup(on_scalar, SIGMOID, 1, 2, 4)
        quantise_weights(SIGMOID, 0, 0)
        quantise_weights(SIGMOID, 1, 0)
        quantise_weights(SIGMOID, 0, 1)
        regroup(on_scalar, SIGMOID, 2, 3, 4)
        nc.scalar.copy(out=bias[:], in_=bias_psum[:, 0:2 * TILES])
        multiply(SIGMOID, 0, 0, 2)
        multiply(SIGMOID, 1, 0, 2)
        multiply(SIGMOID, 0, 2, TILES)
        regroup(on_vector, SIGMOID, 2, 0, 2)
        quantise_weights(SIGMOID, 1, 1)
        quantise_weights(SIGMOID, 2, 0)
        regroup(on_vector, SIGMOID, 2, 2, 3)
        for n in range(TILES):
            gate(TANH, n)
        multiply(SIGMOID, 2, 0, 2)
        multiply(SIGMOID, 1, 2, TILES)
        quantise_weights(SIGMOID, 2, 1)
        multiply(SIGMOID, 2, 2, TILES)

        for n in range(TILES):
            gate(SIGMOID, n)
            product(n)
            transpose_product(n)
        store(on_scalar, 0)
        store(on_scalar, 1)
        store(on_vector, 2)
        store(on_vector, 3)
